import numpy as np
import ml_dtypes


def mxq(x, axis, fmt="e4m3"):
    dtype, down = {"e4m3": (ml_dtypes.float8_e4m3fn, 7), "e5m2": (ml_dtypes.float8_e5m2, 14)}[fmt]
    v = np.moveaxis(np.asarray(x, np.float32).astype(ml_dtypes.bfloat16).astype(np.float64), axis, -1)
    blocks = v.reshape(v.shape[:-1] + (-1, 32))
    amax = np.abs(blocks).max(-1, keepdims=True)
    byte = np.maximum(np.where(amax > 0, np.frexp(amax)[1] - 1 + 127, 0) - down, 1)
    scale = np.exp2(byte - 127.0)
    codes = (blocks / scale).astype(np.float32).astype(dtype).astype(np.float64)
    return np.moveaxis((codes * scale).reshape(v.shape), -1, axis)


WIDE = False


def mx_kscale(k):
    if not WIDE:
        return np.ones(k)
    levels = np.array([10, -10, 5, -5, 0])
    if k % 512:
        return np.exp2(np.random.permutation(np.resize(levels, k // 32))).repeat(32)
    a = np.empty((k // 512, 16))
    for p in range(k // 512):
        a[p, :8] = np.random.permutation(np.resize(levels, 8))
        for g in range(8):
            far = levels[np.abs(levels - a[p, g]) >= 10]
            a[p, g + 8] = far[np.random.randint(len(far))]
    return np.exp2(a.ravel()).repeat(32)


BF16 = ml_dtypes.bfloat16


def bf(x):
    return np.asarray(x, np.float32).astype(BF16)


def f64(x):
    return np.asarray(x).astype(np.float64)


B, N, E, H, NOPE, VDIM, ROPE, QR, KVR = 4, 256, 2048, 16, 128, 128, 128, 512, 512
QH = NOPE + ROPE
BASE = 10000.0


def rope(v):
    d = v.shape[-1]
    n = v.shape[-2]
    theta = BASE ** (-2.0 * np.arange(d // 2) / d)
    ang = np.arange(n)[:, None] * theta[None, :]
    cos, sin = np.cos(ang), np.sin(ang)
    v1, v2 = v[..., 0::2], v[..., 1::2]
    return np.stack([v1 * cos - v2 * sin, v1 * sin + v2 * cos], axis=-1).reshape(v.shape)


def setup_inputs():
    s, t = mx_kscale(E), mx_kscale(QR)
    return {"x": bf(np.random.standard_normal((B, N, E)) * s),
            "Wqa": bf(np.random.standard_normal((E, QR)) / np.sqrt(E) / s[:, None] * t),
            "Wqb": bf(np.random.standard_normal((QR, H * QH)) / np.sqrt(QR) / t[:, None])}


def reference(x, Wqa, Wqb):
    cq = mxq(f64(x), 2, "e4m3") @ mxq(f64(Wqa), 0, "e4m3")
    q = mxq(cq, 2, "e4m3") @ mxq(f64(Wqb), 0, "e4m3")
    q = q.reshape(B, N, H, QH).transpose(0, 2, 1, 3)
    return np.concatenate([q[..., :NOPE], rope(q[..., NOPE:])], axis=-1)

@@ -1,0 +1,318 @@
+import math
+from contextlib import ExitStack
+
+import concourse.masks as masks
+import concourse.mybir as mybir
+
+F32 = mybir.dt.float32
+BF16 = mybir.dt.bfloat16
+U32 = mybir.dt.uint32
+U8 = mybir.dt.uint8
+I32 = mybir.dt.int32
+FP8X4 = mybir.dt.float8_e4m3fn_x4
+ALU = mybir.AluOpType
+ACT = mybir.ActivationFunctionType
+
+P = 128
+B, N, E, H, QR = 4, 256, 2048, 16, 512
+NOPE, ROPE = 128, 128
+QH = NOPE + ROPE
+BASE = 10000.0
+S = 8
+G1 = E // 512
+HG = 4
+NG = H // HG
+FREQ = ROPE // 2
+
+FLOPS = 2 * B * N * E * QR + 2 * B * N * QR * H * QH
+
+
+def tile_multilatentattention_pa_kernel(tc, x, Wqa, Wqb, out):
+    nc = tc.nc
+    with ExitStack() as ctx:
+        keep = ctx.enter_context(tc.tile_pool(name="keep", bufs=1))
+        work = ctx.enter_context(tc.tile_pool(name="work", bufs=2))
+        psum = ctx.enter_context(tc.psum_pool(name="psum", bufs=8))
+        ctx.enter_context(tc.manual_schedule())
+
+        wa_codes = [keep.tile([P, QR], U32, name="wa_codes%d" % g, align_bytes=64) for g in range(G1)]
+        wa_scale = [keep.tile([P, QR], U8, name="wa_scale%d" % g, align_bytes=64) for g in range(G1)]
+        x_codes = [keep.tile([P, G1 * P], U32, name="x_codes%d" % s, align_bytes=64) for s in range(S)]
+        x_scale = [keep.tile([P, G1 * P], U8, name="x_scale%d" % s, align_bytes=64) for s in range(S)]
+        cq_codes = [keep.tile([P, P], U32, name="cq_codes%d" % s, align_bytes=64) for s in range(S)]
+        cq_scale = [keep.tile([P, P], U8, name="cq_scale%d" % s, align_bytes=64) for s in range(S)]
+        wb_codes = [keep.tile([P, 512], U32, name="wb_codes%d" % i, align_bytes=64) for i in range(2 * NG)]
+        wb_scale = [keep.tile([P, 512], U8, name="wb_scale%d" % i, align_bytes=64) for i in range(2 * NG)]
+
+        wa_raw = []
+        x_raw = []
+        wb_raw = []
+        x_view = x.rearrange("b (p s) k -> b p s k", s=2)
+
+        def load_wa(half):
+            wa = work.tile([P, 2, 2048], BF16, name="wa_raw%d" % half, tag="raw8", bufs=6)
+            for gg in range(2):
+                g = 2 * half + gg
+                nc.sync.dma_start(
+                    out=wa[:, gg],
+                    in_=Wqa[512 * g : 512 * (g + 1), :].rearrange("(p t) c -> p (t c)", t=4),
+                )
+            wa_raw.append(wa)
+
+        def load_x(sq, pieces):
+            xs = work.tile([P, 2, E], BF16, name="x_raw%d" % sq, tag="raw8", bufs=6)
+            step = 2 // pieces
+            for i in range(pieces):
+                nc.sync.dma_start(
+                    out=xs[:, step * i : step * (i + 1), :],
+                    in_=x_view[sq, :, step * i : step * (i + 1), :],
+                )
+            x_raw.append(xs)
+
+        def load_wb(g):
+            wb = work.tile([P, 4, 1024], BF16, name="wb_raw%d" % g, tag="raw8", bufs=6)
+            nc.sync.dma_start(
+                out=wb[:], in_=Wqb[:, 1024 * g : 1024 * (g + 1)].rearrange("(p t) c -> p t c", t=4)
+            )
+            wb_raw.append(wb)
+
+        load_wa(0)
+        load_wa(1)
+        load_x(0, 2)
+        load_x(1, 1)
+        load_x(2, 1)
+        load_wb(0)
+        load_x(3, 1)
+        load_wb(1)
+        load_wb(2)
+        load_wb(3)
+
+        warm = keep.tile([P, 1], F32, name="warm")
+        nc.vector.memset(warm[:], 0.0)
+        nc.scalar.activation(out=warm[:], in_=warm[:], func=ACT.Sin)
+
+        ident = keep.tile([P, P], F32, name="ident")
+        masks.make_identity(nc, ident[:])
+        pos_i = keep.tile([P, 2], I32, name="pos_i")
+        nc.gpsimd.iota(pos_i[:], pattern=[[1, 2]], base=0, channel_multiplier=2)
+        pos_a = keep.tile([P, 2], F32, name="pos_a")
+        nc.vector.tensor_copy(out=pos_a[:], in_=pos_i[:])
+        nc.vector.tensor_scalar_mul(out=pos_a[:], in0=pos_a[:], scalar1=1.0 / (2.0 * math.pi))
+        theta = keep.tile([P, FREQ], F32, name="theta")
+        nc.vector.memset(theta[:, 0:1], 1.0)
+        for j in range(6):
+            w = 1 << j
+            nc.vector.tensor_scalar_mul(
+                out=theta[:, w : 2 * w], in0=theta[:, 0:w], scalar1=BASE ** (-2.0 * w / ROPE)
+            )
+        scratch = keep.tile([P, 6, 2 * FREQ], F32, name="scratch")
+        turns = scratch[:, 0, :]
+        whole_i = scratch[:, 1, :].bitcast(I32)
+        whole_f = scratch[:, 2, :]
+        turns_c = scratch[:, 3, :]
+        fold_s = scratch[:, 4, :]
+        fold_c = scratch[:, 5, :]
+        planes = keep.tile([P, 4, 2 * FREQ], F32, name="planes")
+        table = keep.tile([P, 2, FREQ, 4], F32, name="table")
+        nc.vector.tensor_tensor(
+            out=turns.rearrange("p (s m) -> p s m", s=2),
+            in0=theta[:].unsqueeze(1).to_broadcast([P, 2, FREQ]),
+            in1=pos_a[:].unsqueeze(2).to_broadcast([P, 2, FREQ]),
+            op=ALU.mult,
+        )
+        nc.vector.tensor_copy(out=whole_i, in_=turns)
+        nc.vector.tensor_copy(out=whole_f, in_=whole_i)
+
+        nc.vector.tensor_tensor(out=turns, in0=turns, in1=whole_f, op=ALU.subtract)
+        nc.vector.tensor_scalar_add(out=turns_c, in0=turns, scalar1=0.25)
+        nc.vector.scalar_tensor_tensor(
+            out=fold_s, in0=turns, scalar=0.5, in1=turns, op0=ALU.is_gt, op1=ALU.subtract
+        )
+        nc.vector.scalar_tensor_tensor(
+            out=fold_c, in0=turns_c, scalar=0.5, in1=turns_c, op0=ALU.is_gt, op1=ALU.subtract
+        )
+        for plane, src, sign in ((0, fold_c, -1.0), (1, fold_s, -1.0), (2, fold_s, 1.0), (3, fold_c, -1.0)):
+            nc.scalar.activation(out=planes[:, plane, :], in_=src, func=ACT.Sin, scale=sign * 2.0 * math.pi)
+
+        def interleave_tables():
+            nc.vector.tensor_copy(
+                out=table[:].rearrange("p s m q -> p (s m) q"), in_=planes[:].rearrange("p q x -> p x q")
+            )
+
+        wa_grouped = []
+
+        def wa_regroup(g):
+            wag = work.tile([P, QR, 4], BF16, name="wag%d" % g, tag="wag", bufs=2, align_bytes=64)
+            nc.vector.tensor_copy(
+                out=wag[:].rearrange("p (c m) t -> p c m t", c=4),
+                in_=wa_raw[g // 2][:, g % 2].rearrange("p (t m c) -> p c m t", t=4, c=4),
+            )
+            wa_grouped.append(wag)
+
+        def wa_quant(g):
+            nc.vector.quantize_mx(
+                out=wa_codes[g][:].bitcast(FP8X4),
+                scales=wa_scale[g][:],
+                in_=wa_grouped[g][:].rearrange("p c t -> p (c t)"),
+            )
+
+        x_grouped = {}
+        cq_grouped = {}
+
+        def transpose_x(s):
+            words = x_raw[s // 2][:].bitcast(F32)
+            xg = work.tile([P, G1, P, 4], BF16, name="xg%d" % s, tag="xg", bufs=3, align_bytes=64)
+            xg_words = xg[:].bitcast(F32)
+            for half in range(2):
+                xt = psum.tile([P, 2, 2, P], F32, name="xt", tag="ps")
+                for gg in range(2):
+                    for u in range(2):
+                        col = 256 * (2 * half + gg)
+                        nc.tensor.transpose(
+                            out=xt[:, gg, u, :], in_=words[:, s % 2, col + u : col + 256 : 2], identity=ident[:]
+                        )
+                nc.scalar.copy(
+                    out=xg_words[:, 2 * half : 2 * half + 2, :, :],
+                    in_=xt[:].rearrange("p g u t -> p g t u"),
+                )
+            x_grouped[s] = xg
+
+        def quant_x(s):
+            nc.vector.quantize_mx(
+                out=x_codes[s][:].bitcast(FP8X4),
+                scales=x_scale[s][:],
+                in_=x_grouped[s][:].rearrange("p g t j -> p (g t j)"),
+            )
+
+        def first_matmul(s):
+            cqp = psum.tile([P, 4, P], F32, name="cqp", tag="ps")
+            for c in range(4):
+                for g in range(G1):
+                    nc.tensor.matmul_mx(
+                        out=cqp[:, c, :],
+                        lhsT=wa_codes[g][:, P * c : P * (c + 1)].bitcast(FP8X4),
+                        lhsT_scale=wa_scale[g][:, P * c : P * (c + 1)],
+                        rhs=x_codes[s][:, P * g : P * (g + 1)].bitcast(FP8X4),
+                        rhs_scale=x_scale[s][:, P * g : P * (g + 1)],
+                        start=(g == 0),
+                        stop=(g == G1 - 1),
+                    )
+            cqg = work.tile([P, P, 4], BF16, name="cqg%d" % s, tag="cqg", bufs=3, align_bytes=64)
+            nc.scalar.copy(out=cqg[:], in_=cqp[:].rearrange("p c t -> p t c"))
+            cq_grouped[s] = cqg
+
+        def quant_cq(s):
+            nc.vector.quantize_mx(
+                out=cq_codes[s][:].bitcast(FP8X4),
+                scales=cq_scale[s][:],
+                in_=cq_grouped[s][:].rearrange("p t c -> p (t c)"),
+            )
+
+        def both(step, j):
+            step(2 * j)
+            step(2 * j + 1)
+
+        wb_grouped = {}
+
+        def wb_regroup(g, kind, copy):
+            wbg = work.tile([P, 512, 4], BF16, name="wbg", tag="wbg", bufs=2, align_bytes=64)
+            src = wb_raw[g][:].rearrange("p t (h k c) -> p k h c t", h=HG, k=2)
+            copy(out=wbg[:].rearrange("p (h c) t -> p h c t", h=HG), in_=src[:, kind])
+            wb_grouped[2 * g + kind] = wbg
+
+        def wb_quant(g, kind):
+            nc.vector.quantize_mx(
+                out=wb_codes[2 * g + kind][:].bitcast(FP8X4),
+                scales=wb_scale[2 * g + kind][:],
+                in_=wb_grouped[2 * g + kind][:].rearrange("p c t -> p (c t)"),
+            )
+
+        out_view = out.rearrange("b h (p s) f -> b p h s f", s=2)
+
+        def second_matmul(g, kind, s):
+            q_ps = psum.tile([P, 512], F32, name="q_ps", tag="ps")
+            nc.tensor.matmul_mx(
+                out=q_ps[:],
+                lhsT=cq_codes[s][:].bitcast(FP8X4),
+                lhsT_scale=cq_scale[s][:],
+                rhs=wb_codes[2 * g + kind][:].bitcast(FP8X4),
+                rhs_scale=wb_scale[2 * g + kind][:],
+                start=True,
+                stop=True,
+            )
+            return q_ps
+
+        def rotate(q_rope, s, products):
+            shape = [P, HG, ROPE, 2]
+            nc.vector.tensor_tensor(
+                out=products[:, :, s % 2, :].rearrange("p h (x e) -> p h x e", e=2),
+                in0=q_rope[:].rearrange("p (h x) -> p h x", h=HG).unsqueeze(3).to_broadcast(shape),
+                in1=table[:, s % 2].rearrange("p m (j e) -> p (m j) e", e=2).unsqueeze(1).to_broadcast(shape),
+                op=ALU.mult,
+            )
+
+        def store(res, g, s0):
+            nc.sync.dma_start(
+                out=out_view[s0 // 2, :, HG * g : HG * (g + 1), :, :], in_=res[:, :, s0 % 4 : s0 % 4 + 2, :]
+            )
+
+        by_scalar = nc.scalar.copy
+        by_vector = nc.vector.tensor_copy
+
+        wa_regroup(0)
+        for g in range(1, G1):
+            wa_regroup(g)
+            wa_quant(g - 1)
+        wa_quant(G1 - 1)
+
+        interleave_tables()
+        both(transpose_x, 0)
+        both(quant_x, 0)
+        both(transpose_x, 1)
+        both(first_matmul, 0)
+        both(quant_x, 1)
+        both(transpose_x, 2)
+        both(first_matmul, 1)
+        wb_regroup(0, 1, by_vector)
+        both(quant_cq, 0)
+        both(quant_x, 2)
+        both(transpose_x, 3)
+        both(first_matmul, 2)
+        wb_regroup(0, 0, by_vector)
+        wb_quant(0, 1)
+        both(quant_cq, 1)
+        wb_quant(0, 0)
+        both(quant_x, 3)
+        both(first_matmul, 3)
+        both(quant_cq, 2)
+        both(quant_cq, 3)
+
+        for g in range(NG):
+            for sh in range(2):
+                res = work.tile([P, HG, 4, QH], F32, name="res", tag="res", bufs=4)
+                ropes = []
+                for sl in range(4):
+                    s = 4 * sh + sl
+                    ropes.append(second_matmul(g, 1, s))
+                    q_nope = second_matmul(g, 0, s)
+                    nc.scalar.copy(
+                        out=res[:, :, sl, 0:NOPE], in_=q_nope[:].rearrange("p (h c) -> p h c", h=HG)
+                    )
+                if sh == 0 and g + 1 < NG:
+                    wb_regroup(g + 1, 1, by_scalar)
+                    wb_regroup(g + 1, 0, by_scalar)
+                for pair in range(2):
+                    products = work.tile([P, HG, 2, 2 * ROPE], F32, name="products", tag="products", bufs=3)
+                    for k in range(2):
+                        rotate(ropes[2 * pair + k], 4 * sh + 2 * pair + k, products)
+                    terms = products[:].rearrange("p h k (m j e) -> p (h k) m j e", j=2, e=2)
+                    nc.gpsimd.tensor_tensor(
+                        out=res[:, :, 2 * pair : 2 * pair + 2, NOPE:QH],
+                        in0=terms[:, :, :, 0, :],
+                        in1=terms[:, :, :, 1, :],
+                        op=ALU.add,
+                    )
+                    store(res, g, 4 * sh + 2 * pair)
+                    if pair == 0 and sh == 1 and g + 1 < NG:
+                        wb_quant(g + 1, 1)
+                        wb_quant(g + 1, 0)

@@ -120,34 +120,39 @@ def tile_multilatentattention_pa_kernel(tc, x, Wqa, Wqb, out):
             in1=pos_a[:].unsqueeze(2).to_broadcast([P, 2, FREQ]),
             op=ALU.mult,
         )
-        nc.vector.tensor_copy(out=whole_i, in_=turns)
-        nc.vector.tensor_copy(out=whole_f, in_=whole_i)
 
-        nc.vector.tensor_tensor(out=turns, in0=turns, in1=whole_f, op=ALU.subtract)
-        nc.vector.tensor_scalar_add(out=turns_c, in0=turns, scalar1=0.25)
-        nc.vector.scalar_tensor_tensor(
-            out=fold_s, in0=turns, scalar=0.5, in1=turns, op0=ALU.is_gt, op1=ALU.subtract
-        )
-        nc.vector.scalar_tensor_tensor(
-            out=fold_c, in0=turns_c, scalar=0.5, in1=turns_c, op0=ALU.is_gt, op1=ALU.subtract
-        )
-        for plane, src, sign in ((0, fold_c, -1.0), (1, fold_s, -1.0), (2, fold_s, 1.0), (3, fold_c, -1.0)):
-            nc.scalar.activation(out=planes[:, plane, :], in_=src, func=ACT.Sin, scale=sign * 2.0 * math.pi)
+        def angle_whole():
+            nc.vector.tensor_copy(out=whole_i, in_=turns)
+
+        def angle_fraction():
+            nc.vector.tensor_copy(out=whole_f, in_=whole_i)
+            nc.vector.tensor_tensor(out=turns, in0=turns, in1=whole_f, op=ALU.subtract)
+
+        def angle_fold():
+            nc.vector.tensor_scalar_add(out=turns_c, in0=turns, scalar1=0.25)
+            for fold, src in ((fold_s, turns), (fold_c, turns_c)):
+                nc.vector.scalar_tensor_tensor(
+                    out=fold, in0=src, scalar=0.5, in1=src, op0=ALU.is_gt, op1=ALU.subtract
+                )
+
+        def angle_sin():
+            for plane, src, sign in ((0, fold_c, -1.0), (1, fold_s, -1.0), (2, fold_s, 1.0), (3, fold_c, -1.0)):
+                nc.scalar.activation(out=planes[:, plane, :], in_=src, func=ACT.Sin, scale=sign * 2.0 * math.pi)
 
         def interleave_tables():
             nc.vector.tensor_copy(
                 out=table[:].rearrange("p s m q -> p (s m) q"), in_=planes[:].rearrange("p q x -> p x q")
             )
 
-        wa_grouped = []
+        wa_grouped = {}
 
-        def wa_regroup(g):
-            wag = work.tile([P, QR, 4], BF16, name="wag%d" % g, tag="wag", bufs=2, align_bytes=64)
-            nc.vector.tensor_copy(
+        def wa_regroup(g, copy):
+            wag = work.tile([P, QR, 4], BF16, name="wag%d" % g, tag="wag", bufs=3, align_bytes=64)
+            copy(
                 out=wag[:].rearrange("p (c m) t -> p c m t", c=4),
                 in_=wa_raw[g // 2][:, g % 2].rearrange("p (t m c) -> p c m t", t=4, c=4),
             )
-            wa_grouped.append(wag)
+            wa_grouped[g] = wag
 
         def wa_quant(g):
             nc.vector.quantize_mx(
@@ -259,18 +264,25 @@ def tile_multilatentattention_pa_kernel(tc, x, Wqa, Wqb, out):
         by_scalar = nc.scalar.copy
         by_vector = nc.vector.tensor_copy
 
-        wa_regroup(0)
-        for g in range(1, G1):
-            wa_regroup(g)
-            wa_quant(g - 1)
-        wa_quant(G1 - 1)
+        wa_regroup(0, by_vector)
+        wa_regroup(1, by_scalar)
+        angle_whole()
+        wa_quant(0)
+        wa_regroup(2, by_vector)
+        wa_quant(1)
+        wa_regroup(3, by_vector)
+        wa_quant(2)
+        angle_fraction()
+        wa_quant(3)
 
-        interleave_tables()
         both(transpose_x, 0)
         both(quant_x, 0)
+        angle_fold()
+        angle_sin()
         both(transpose_x, 1)
         both(first_matmul, 0)
         both(quant_x, 1)
+        interleave_tables()
         both(transpose_x, 2)
         both(first_matmul, 1)
         wb_regroup(0, 1, by_vector)

@@ -79,10 +79,10 @@ def tile_multilatentattention_pa_kernel(tc, x, Wqa, Wqb, out):
         load_wa(0)
         load_wa(1)
         load_x(0, 2)
-        load_x(1, 1)
-        load_x(2, 1)
+        load_x(1, 2)
+        load_x(2, 2)
         load_wb(0)
-        load_x(3, 1)
+        load_x(3, 2)
         load_wb(1)
         load_wb(2)
         load_wb(3)
@@ -149,8 +149,8 @@ def tile_multilatentattention_pa_kernel(tc, x, Wqa, Wqb, out):
         def wa_regroup(g, copy):
             wag = work.tile([P, QR, 4], BF16, name="wag%d" % g, tag="wag", bufs=3, align_bytes=64)
             copy(
-                out=wag[:].rearrange("p (c m) t -> p c m t", c=4),
-                in_=wa_raw[g // 2][:, g % 2].rearrange("p (t m c) -> p c m t", t=4, c=4),
+                out=wag[:].rearrange("p (c m) t -> p m c t", c=4),
+                in_=wa_raw[g // 2][:, g % 2].rearrange("p (t m c) -> p m c t", t=4, c=4),
             )
             wa_grouped[g] = wag
 
@@ -277,9 +277,9 @@ def tile_multilatentattention_pa_kernel(tc, x, Wqa, Wqb, out):
 
         both(transpose_x, 0)
         both(quant_x, 0)
+        both(transpose_x, 1)
         angle_fold()
         angle_sin()
-        both(transpose_x, 1)
         both(first_matmul, 0)
         both(quant_x, 1)
         interleave_tables()

@@ -213,10 +213,6 @@ def tile_multilatentattention_pa_kernel(tc, x, Wqa, Wqb, out):
                 in_=cq_grouped[s][:].rearrange("p t c -> p (t c)"),
             )
 
-        def both(step, j):
-            step(2 * j)
-            step(2 * j + 1)
-
         wb_grouped = {}
 
         def wb_regroup(g, kind, copy):
@@ -247,19 +243,50 @@ def tile_multilatentattention_pa_kernel(tc, x, Wqa, Wqb, out):
             )
             return q_ps
 
-        def rotate(q_rope, s, products):
+        rope_banks = {}
+        results = {}
+        stores_left = {}
+
+        def pair_tiles(g, j):
+            if (g, j) not in results:
+                results[g, j] = (
+                    work.tile([P, HG, 2, QH], F32, name="res", tag="res", bufs=6),
+                    work.tile([P, HG, 2, 2 * ROPE], F32, name="products", tag="products", bufs=3),
+                )
+                stores_left[g, j] = 3
+            return results[g, j]
+
+        def store_when_done(g, j):
+            stores_left[g, j] -= 1
+            if stores_left[g, j] == 0:
+                nc.sync.dma_start(out=out_view[j, :, HG * g : HG * (g + 1), :, :], in_=results[g, j][0][:])
+
+        def make_rope(g, s):
+            rope_banks[g, s] = second_matmul(g, 1, s)
+
+        def make_nope(g, s):
+            res = pair_tiles(g, s // 2)[0]
+            q_nope = second_matmul(g, 0, s)
+            nc.scalar.copy(out=res[:, :, s % 2, 0:NOPE], in_=q_nope[:].rearrange("p (h c) -> p h c", h=HG))
+            store_when_done(g, s // 2)
+
+        def rotate(g, s):
+            products = pair_tiles(g, s // 2)[1]
             shape = [P, HG, ROPE, 2]
             nc.vector.tensor_tensor(
                 out=products[:, :, s % 2, :].rearrange("p h (x e) -> p h x e", e=2),
-                in0=q_rope[:].rearrange("p (h x) -> p h x", h=HG).unsqueeze(3).to_broadcast(shape),
+                in0=rope_banks[g, s][:].rearrange("p (h x) -> p h x", h=HG).unsqueeze(3).to_broadcast(shape),
                 in1=table[:, s % 2].rearrange("p m (j e) -> p (m j) e", e=2).unsqueeze(1).to_broadcast(shape),
                 op=ALU.mult,
             )
 
-        def store(res, g, s0):
-            nc.sync.dma_start(
-                out=out_view[s0 // 2, :, HG * g : HG * (g + 1), :, :], in_=res[:, :, s0 % 4 : s0 % 4 + 2, :]
+        def add(g, j, eng):
+            res, products = pair_tiles(g, j)
+            terms = products[:].rearrange("p h k (m j e) -> p (h k) m j e", j=2, e=2)
+            eng.tensor_tensor(
+                out=res[:, :, :, NOPE:QH], in0=terms[:, :, :, 0, :], in1=terms[:, :, :, 1, :], op=ALU.add
             )
+            store_when_done(g, j)
 
         by_scalar = nc.scalar.copy
         by_vector = nc.vector.tensor_copy
@@ -274,57 +301,166 @@ def tile_multilatentattention_pa_kernel(tc, x, Wqa, Wqb, out):
         wa_quant(2)
         angle_fraction()
         wa_quant(3)
-
-        both(transpose_x, 0)
-        both(quant_x, 0)
-        both(transpose_x, 1)
+        transpose_x(0)
+        transpose_x(1)
+        quant_x(0)
+        quant_x(1)
+        transpose_x(2)
+        transpose_x(3)
         angle_fold()
         angle_sin()
-        both(first_matmul, 0)
-        both(quant_x, 1)
+        first_matmul(0)
+        first_matmul(1)
+        quant_x(2)
+        quant_x(3)
         interleave_tables()
-        both(transpose_x, 2)
-        both(first_matmul, 1)
+        transpose_x(4)
+        transpose_x(5)
+        first_matmul(2)
+        first_matmul(3)
         wb_regroup(0, 1, by_vector)
-        both(quant_cq, 0)
-        both(quant_x, 2)
-        both(transpose_x, 3)
-        both(first_matmul, 2)
-        wb_regroup(0, 0, by_vector)
+        quant_cq(0)
+        quant_cq(1)
         wb_quant(0, 1)
-        both(quant_cq, 1)
+        quant_x(4)
+        quant_x(5)
+        make_rope(0, 0)
+        make_rope(0, 1)
+        transpose_x(6)
+        wb_regroup(0, 0, by_vector)
+        quant_cq(2)
+        quant_cq(3)
+        transpose_x(7)
         wb_quant(0, 0)
-        both(quant_x, 3)
-        both(first_matmul, 3)
-        both(quant_cq, 2)
-        both(quant_cq, 3)
-
-        for g in range(NG):
-            for sh in range(2):
-                res = work.tile([P, HG, 4, QH], F32, name="res", tag="res", bufs=4)
-                ropes = []
-                for sl in range(4):
-                    s = 4 * sh + sl
-                    ropes.append(second_matmul(g, 1, s))
-                    q_nope = second_matmul(g, 0, s)
-                    nc.scalar.copy(
-                        out=res[:, :, sl, 0:NOPE], in_=q_nope[:].rearrange("p (h c) -> p h c", h=HG)
-                    )
-                if sh == 0 and g + 1 < NG:
-                    wb_regroup(g + 1, 1, by_scalar)
-                    wb_regroup(g + 1, 0, by_scalar)
-                for pair in range(2):
-                    products = work.tile([P, HG, 2, 2 * ROPE], F32, name="products", tag="products", bufs=3)
-                    for k in range(2):
-                        rotate(ropes[2 * pair + k], 4 * sh + 2 * pair + k, products)
-                    terms = products[:].rearrange("p h k (m j e) -> p (h k) m j e", j=2, e=2)
-                    nc.gpsimd.tensor_tensor(
-                        out=res[:, :, 2 * pair : 2 * pair + 2, NOPE:QH],
-                        in0=terms[:, :, :, 0, :],
-                        in1=terms[:, :, :, 1, :],
-                        op=ALU.add,
-                    )
-                    store(res, g, 4 * sh + 2 * pair)
-                    if pair == 0 and sh == 1 and g + 1 < NG:
-                        wb_quant(g + 1, 1)
-                        wb_quant(g + 1, 0)
+        rotate(0, 0)
+        first_matmul(4)
+        rotate(0, 1)
+        make_rope(0, 2)
+        first_matmul(5)
+        make_rope(0, 3)
+        make_nope(0, 0)
+        make_nope(0, 1)
+        add(0, 0, nc.gpsimd)
+        quant_x(6)
+        quant_x(7)
+        first_matmul(6)
+        rotate(0, 2)
+        rotate(0, 3)
+        quant_cq(4)
+        quant_cq(5)
+        make_rope(0, 4)
+        make_rope(0, 5)
+        first_matmul(7)
+        add(0, 1, nc.gpsimd)
+        make_nope(0, 2)
+        make_nope(0, 3)
+        wb_regroup(1, 1, by_scalar)
+        rotate(0, 4)
+        rotate(0, 5)
+        quant_cq(6)
+        quant_cq(7)
+        make_rope(0, 6)
+        make_rope(0, 7)
+        add(0, 2, nc.gpsimd)
+        rotate(0, 6)
+        rotate(0, 7)
+        wb_regroup(1, 0, by_vector)
+        wb_quant(1, 1)
+        wb_quant(1, 0)
+        make_nope(0, 4)
+        make_nope(0, 5)
+        make_nope(0, 6)
+        make_nope(0, 7)
+        add(0, 3, nc.gpsimd)
+        make_rope(1, 0)
+        make_rope(1, 1)
+        rotate(1, 0)
+        make_nope(1, 0)
+        make_rope(1, 2)
+        rotate(1, 1)
+        make_nope(1, 1)
+        make_rope(1, 3)
+        add(1, 0, nc.gpsimd)
+        wb_regroup(2, 1, by_scalar)
+        rotate(1, 2)
+        make_nope(1, 2)
+        make_rope(1, 4)
+        rotate(1, 3)
+        make_nope(1, 3)
+        make_rope(1, 5)
+        add(1, 1, nc.gpsimd)
+        wb_regroup(2, 0, by_scalar)
+        rotate(1, 4)
+        make_nope(1, 4)
+        make_rope(1, 6)
+        rotate(1, 5)
+        make_nope(1, 5)
+        make_rope(1, 7)
+        add(1, 2, nc.gpsimd)
+        rotate(1, 6)
+        make_nope(1, 6)
+        rotate(1, 7)
+        make_nope(1, 7)
+        add(1, 3, nc.gpsimd)
+        wb_quant(2, 1)
+        wb_quant(2, 0)
+        make_rope(2, 0)
+        make_rope(2, 1)
+        rotate(2, 0)
+        make_nope(2, 0)
+        make_rope(2, 2)
+        rotate(2, 1)
+        make_nope(2, 1)
+        make_rope(2, 3)
+        add(2, 0, nc.gpsimd)
+        wb_regroup(3, 1, by_scalar)
+        rotate(2, 2)
+        make_nope(2, 2)
+        make_rope(2, 4)
+        rotate(2, 3)
+        make_nope(2, 3)
+        make_rope(2, 5)
+        add(2, 1, nc.gpsimd)
+        wb_regroup(3, 0, by_scalar)
+        rotate(2, 4)
+        make_nope(2, 4)
+        make_rope(2, 6)
+        rotate(2, 5)
+        make_nope(2, 5)
+        make_rope(2, 7)
+        add(2, 2, nc.gpsimd)
+        rotate(2, 6)
+        make_nope(2, 6)
+        rotate(2, 7)
+        make_nope(2, 7)
+        add(2, 3, nc.gpsimd)
+        wb_quant(3, 1)
+        wb_quant(3, 0)
+        make_rope(3, 0)
+        make_rope(3, 1)
+        rotate(3, 0)
+        make_nope(3, 0)
+        make_rope(3, 2)
+        rotate(3, 1)
+        make_nope(3, 1)
+        make_rope(3, 3)
+        add(3, 0, nc.gpsimd)
+        rotate(3, 2)
+        make_nope(3, 2)
+        make_rope(3, 4)
+        rotate(3, 3)
+        make_nope(3, 3)
+        make_rope(3, 5)
+        add(3, 1, nc.gpsimd)
+        rotate(3, 4)
+        make_nope(3, 4)
+        make_rope(3, 6)
+        rotate(3, 5)
+        make_nope(3, 5)
+        make_rope(3, 7)
+        add(3, 2, nc.gpsimd)
+        rotate(3, 6)
+        make_nope(3, 6)
+        rotate(3, 7)
+        make_nope(3, 7)
+        add(3, 3, nc.gpsimd)

@@ -217,8 +217,8 @@ def tile_multilatentattention_pa_kernel(tc, x, Wqa, Wqb, out):
 
         def wb_regroup(g, kind, copy):
             wbg = work.tile([P, 512, 4], BF16, name="wbg", tag="wbg", bufs=2, align_bytes=64)
-            src = wb_raw[g][:].rearrange("p t (h k c) -> p k h c t", h=HG, k=2)
-            copy(out=wbg[:].rearrange("p (h c) t -> p h c t", h=HG), in_=src[:, kind])
+            src = wb_raw[g][:].rearrange("p t (h k c i) -> p k h c t i", h=HG, k=2, i=4)
+            copy(out=wbg[:].rearrange("p (h c i) t -> p h c t i", h=HG, i=4), in_=src[:, kind])
             wb_grouped[2 * g + kind] = wbg
 
         def wb_quant(g, kind):
@@ -297,7 +297,7 @@ def tile_multilatentattention_pa_kernel(tc, x, Wqa, Wqb, out):
         wa_quant(0)
         wa_regroup(2, by_vector)
         wa_quant(1)
-        wa_regroup(3, by_vector)
+        wa_regroup(3, by_scalar)
         wa_quant(2)
         angle_fraction()
         wa_quant(3)

@@ -80,8 +80,8 @@ def tile_multilatentattention_pa_kernel(tc, x, Wqa, Wqb, out):
         load_wa(1)
         load_x(0, 2)
         load_x(1, 2)
-        load_x(2, 2)
         load_wb(0)
+        load_x(2, 2)
         load_x(3, 2)
         load_wb(1)
         load_wb(2)

import math
from contextlib import ExitStack

import concourse.masks as masks
import concourse.mybir as mybir

F32 = mybir.dt.float32
BF16 = mybir.dt.bfloat16
U32 = mybir.dt.uint32
U8 = mybir.dt.uint8
I32 = mybir.dt.int32
FP8X4 = mybir.dt.float8_e4m3fn_x4
ALU = mybir.AluOpType
ACT = mybir.ActivationFunctionType

P = 128
B, N, E, H, QR = 4, 256, 2048, 16, 512
NOPE, ROPE = 128, 128
QH = NOPE + ROPE
BASE = 10000.0
S = 8
G1 = E // 512
HG = 4
NG = H // HG
FREQ = ROPE // 2

FLOPS = 2 * B * N * E * QR + 2 * B * N * QR * H * QH


def tile_multilatentattention_pa_kernel(tc, x, Wqa, Wqb, out):
    nc = tc.nc
    with ExitStack() as ctx:
        keep = ctx.enter_context(tc.tile_pool(name="keep", bufs=1))
        work = ctx.enter_context(tc.tile_pool(name="work", bufs=2))
        psum = ctx.enter_context(tc.psum_pool(name="psum", bufs=8))
        ctx.enter_context(tc.manual_schedule())

        wa_codes = [keep.tile([P, QR], U32, name="wa_codes%d" % g, align_bytes=64) for g in range(G1)]
        wa_scale = [keep.tile([P, QR], U8, name="wa_scale%d" % g, align_bytes=64) for g in range(G1)]
        x_codes = [keep.tile([P, G1 * P], U32, name="x_codes%d" % s, align_bytes=64) for s in range(S)]
        x_scale = [keep.tile([P, G1 * P], U8, name="x_scale%d" % s, align_bytes=64) for s in range(S)]
        cq_codes = [keep.tile([P, P], U32, name="cq_codes%d" % s, align_bytes=64) for s in range(S)]
        cq_scale = [keep.tile([P, P], U8, name="cq_scale%d" % s, align_bytes=64) for s in range(S)]
        wb_codes = [keep.tile([P, 512], U32, name="wb_codes%d" % i, align_bytes=64) for i in range(2 * NG)]
        wb_scale = [keep.tile([P, 512], U8, name="wb_scale%d" % i, align_bytes=64) for i in range(2 * NG)]

        wa_raw = []
        x_raw = []
        wb_raw = []
        x_view = x.rearrange("b (p s) k -> b p s k", s=2)

        def load_wa(half):
            wa = work.tile([P, 2, 2048], BF16, name="wa_raw%d" % half, tag="raw8", bufs=6)
            for gg in range(2):
                g = 2 * half + gg
                nc.sync.dma_start(
                    out=wa[:, gg],
                    in_=Wqa[512 * g : 512 * (g + 1), :].rearrange("(p t) c -> p (t c)", t=4),
                )
            wa_raw.append(wa)

        def load_x(sq, pieces):
            xs = work.tile([P, 2, E], BF16, name="x_raw%d" % sq, tag="raw8", bufs=6)
            step = 2 // pieces
            for i in range(pieces):
                nc.sync.dma_start(
                    out=xs[:, step * i : step * (i + 1), :],
                    in_=x_view[sq, :, step * i : step * (i + 1), :],
                )
            x_raw.append(xs)

        def load_wb(g):
            wb = work.tile([P, 4, 1024], BF16, name="wb_raw%d" % g, tag="raw8", bufs=6)
            nc.sync.dma_start(
                out=wb[:], in_=Wqb[:, 1024 * g : 1024 * (g + 1)].rearrange("(p t) c -> p t c", t=4)
            )
            wb_raw.append(wb)

        load_wa(0)
        load_wa(1)
        load_x(0, 2)
        load_x(1, 2)
        load_wb(0)
        load_x(2, 2)
        load_x(3, 2)
        load_wb(1)
        load_wb(2)
        load_wb(3)

        warm = keep.tile([P, 1], F32, name="warm")
        nc.vector.memset(warm[:], 0.0)
        nc.scalar.activation(out=warm[:], in_=warm[:], func=ACT.Sin)

        ident = keep.tile([P, P], F32, name="ident")
        masks.make_identity(nc, ident[:])
        pos_i = keep.tile([P, 2], I32, name="pos_i")
        nc.gpsimd.iota(pos_i[:], pattern=[[1, 2]], base=0, channel_multiplier=2)
        pos_a = keep.tile([P, 2], F32, name="pos_a")
        nc.vector.tensor_copy(out=pos_a[:], in_=pos_i[:])
        nc.vector.tensor_scalar_mul(out=pos_a[:], in0=pos_a[:], scalar1=1.0 / (2.0 * math.pi))
        theta = keep.tile([P, FREQ], F32, name="theta")
        nc.vector.memset(theta[:, 0:1], 1.0)
        for j in range(6):
            w = 1 << j
            nc.vector.tensor_scalar_mul(
                out=theta[:, w : 2 * w], in0=theta[:, 0:w], scalar1=BASE ** (-2.0 * w / ROPE)
            )
        scratch = keep.tile([P, 6, 2 * FREQ], F32, name="scratch")
        turns = scratch[:, 0, :]
        whole_i = scratch[:, 1, :].bitcast(I32)
        whole_f = scratch[:, 2, :]
        turns_c = scratch[:, 3, :]
        fold_s = scratch[:, 4, :]
        fold_c = scratch[:, 5, :]
        planes = keep.tile([P, 4, 2 * FREQ], F32, name="planes")
        table = keep.tile([P, 2, FREQ, 4], F32, name="table")
        nc.vector.tensor_tensor(
            out=turns.rearrange("p (s m) -> p s m", s=2),
            in0=theta[:].unsqueeze(1).to_broadcast([P, 2, FREQ]),
            in1=pos_a[:].unsqueeze(2).to_broadcast([P, 2, FREQ]),
            op=ALU.mult,
        )

        def angle_whole():
            nc.vector.tensor_copy(out=whole_i, in_=turns)

        def angle_fraction():
            nc.vector.tensor_copy(out=whole_f, in_=whole_i)
            nc.vector.tensor_tensor(out=turns, in0=turns, in1=whole_f, op=ALU.subtract)

        def angle_fold():
            nc.vector.tensor_scalar_add(out=turns_c, in0=turns, scalar1=0.25)
            for fold, src in ((fold_s, turns), (fold_c, turns_c)):
                nc.vector.scalar_tensor_tensor(
                    out=fold, in0=src, scalar=0.5, in1=src, op0=ALU.is_gt, op1=ALU.subtract
                )

        def angle_sin():
            for plane, src, sign in ((0, fold_c, -1.0), (1, fold_s, -1.0), (2, fold_s, 1.0), (3, fold_c, -1.0)):
                nc.scalar.activation(out=planes[:, plane, :], in_=src, func=ACT.Sin, scale=sign * 2.0 * math.pi)

        def interleave_tables():
            nc.vector.tensor_copy(
                out=table[:].rearrange("p s m q -> p (s m) q"), in_=planes[:].rearrange("p q x -> p x q")
            )

        wa_grouped = {}

        def wa_regroup(g, copy):
            wag = work.tile([P, QR, 4], BF16, name="wag%d" % g, tag="wag", bufs=3, align_bytes=64)
            copy(
                out=wag[:].rearrange("p (c m) t -> p m c t", c=4),
                in_=wa_raw[g // 2][:, g % 2].rearrange("p (t m c) -> p m c t", t=4, c=4),
            )
            wa_grouped[g] = wag

        def wa_quant(g):
            nc.vector.quantize_mx(
                out=wa_codes[g][:].bitcast(FP8X4),
                scales=wa_scale[g][:],
                in_=wa_grouped[g][:].rearrange("p c t -> p (c t)"),
            )

        x_grouped = {}
        cq_grouped = {}

        def transpose_x(s):
            words = x_raw[s // 2][:].bitcast(F32)
            xg = work.tile([P, G1, P, 4], BF16, name="xg%d" % s, tag="xg", bufs=3, align_bytes=64)
            xg_words = xg[:].bitcast(F32)
            for half in range(2):
                xt = psum.tile([P, 2, 2, P], F32, name="xt", tag="ps")
                for gg in range(2):
                    for u in range(2):
                        col = 256 * (2 * half + gg)
                        nc.tensor.transpose(
                            out=xt[:, gg, u, :], in_=words[:, s % 2, col + u : col + 256 : 2], identity=ident[:]
                        )
                nc.scalar.copy(
                    out=xg_words[:, 2 * half : 2 * half + 2, :, :],
                    in_=xt[:].rearrange("p g u t -> p g t u"),
                )
            x_grouped[s] = xg

        def quant_x(s):
            nc.vector.quantize_mx(
                out=x_codes[s][:].bitcast(FP8X4),
                scales=x_scale[s][:],
                in_=x_grouped[s][:].rearrange("p g t j -> p (g t j)"),
            )

        def first_matmul(s):
            cqp = psum.tile([P, 4, P], F32, name="cqp", tag="ps")
            for c in range(4):
                for g in range(G1):
                    nc.tensor.matmul_mx(
                        out=cqp[:, c, :],
                        lhsT=wa_codes[g][:, P * c : P * (c + 1)].bitcast(FP8X4),
                        lhsT_scale=wa_scale[g][:, P * c : P * (c + 1)],
                        rhs=x_codes[s][:, P * g : P * (g + 1)].bitcast(FP8X4),
                        rhs_scale=x_scale[s][:, P * g : P * (g + 1)],
                        start=(g == 0),
                        stop=(g == G1 - 1),
                    )
            cqg = work.tile([P, P, 4], BF16, name="cqg%d" % s, tag="cqg", bufs=3, align_bytes=64)
            nc.scalar.copy(out=cqg[:], in_=cqp[:].rearrange("p c t -> p t c"))
            cq_grouped[s] = cqg

        def quant_cq(s):
            nc.vector.quantize_mx(
                out=cq_codes[s][:].bitcast(FP8X4),
                scales=cq_scale[s][:],
                in_=cq_grouped[s][:].rearrange("p t c -> p (t c)"),
            )

        wb_grouped = {}

        def wb_regroup(g, kind, copy):
            wbg = work.tile([P, 512, 4], BF16, name="wbg", tag="wbg", bufs=2, align_bytes=64)
            src = wb_raw[g][:].rearrange("p t (h k c i) -> p k h c t i", h=HG, k=2, i=4)
            copy(out=wbg[:].rearrange("p (h c i) t -> p h c t i", h=HG, i=4), in_=src[:, kind])
            wb_grouped[2 * g + kind] = wbg

        def wb_quant(g, kind):
            nc.vector.quantize_mx(
                out=wb_codes[2 * g + kind][:].bitcast(FP8X4),
                scales=wb_scale[2 * g + kind][:],
                in_=wb_grouped[2 * g + kind][:].rearrange("p c t -> p (c t)"),
            )

        out_view = out.rearrange("b h (p s) f -> b p h s f", s=2)

        def second_matmul(g, kind, s):
            q_ps = psum.tile([P, 512], F32, name="q_ps", tag="ps")
            nc.tensor.matmul_mx(
                out=q_ps[:],
                lhsT=cq_codes[s][:].bitcast(FP8X4),
                lhsT_scale=cq_scale[s][:],
                rhs=wb_codes[2 * g + kind][:].bitcast(FP8X4),
                rhs_scale=wb_scale[2 * g + kind][:],
                start=True,
                stop=True,
            )
            return q_ps

        rope_banks = {}
        results = {}
        stores_left = {}

        def pair_tiles(g, j):
            if (g, j) not in results:
                results[g, j] = (
                    work.tile([P, HG, 2, QH], F32, name="res", tag="res", bufs=6),
                    work.tile([P, HG, 2, 2 * ROPE], F32, name="products", tag="products", bufs=3),
                )
                stores_left[g, j] = 3
            return results[g, j]

        def store_when_done(g, j):
            stores_left[g, j] -= 1
            if stores_left[g, j] == 0:
                nc.sync.dma_start(out=out_view[j, :, HG * g : HG * (g + 1), :, :], in_=results[g, j][0][:])

        def make_rope(g, s):
            rope_banks[g, s] = second_matmul(g, 1, s)

        def make_nope(g, s):
            res = pair_tiles(g, s // 2)[0]
            q_nope = second_matmul(g, 0, s)
            nc.scalar.copy(out=res[:, :, s % 2, 0:NOPE], in_=q_nope[:].rearrange("p (h c) -> p h c", h=HG))
            store_when_done(g, s // 2)

        def rotate(g, s):
            products = pair_tiles(g, s // 2)[1]
            shape = [P, HG, ROPE, 2]
            nc.vector.tensor_tensor(
                out=products[:, :, s % 2, :].rearrange("p h (x e) -> p h x e", e=2),
                in0=rope_banks[g, s][:].rearrange("p (h x) -> p h x", h=HG).unsqueeze(3).to_broadcast(shape),
                in1=table[:, s % 2].rearrange("p m (j e) -> p (m j) e", e=2).unsqueeze(1).to_broadcast(shape),
                op=ALU.mult,
            )

        def add(g, j, eng):
            res, products = pair_tiles(g, j)
            terms = products[:].rearrange("p h k (m j e) -> p (h k) m j e", j=2, e=2)
            eng.tensor_tensor(
                out=res[:, :, :, NOPE:QH], in0=terms[:, :, :, 0, :], in1=terms[:, :, :, 1, :], op=ALU.add
            )
            store_when_done(g, j)

        by_scalar = nc.scalar.copy
        by_vector = nc.vector.tensor_copy

        wa_regroup(0, by_vector)
        wa_regroup(1, by_scalar)
        angle_whole()
        wa_quant(0)
        wa_regroup(2, by_vector)
        wa_quant(1)
        wa_regroup(3, by_scalar)
        wa_quant(2)
        angle_fraction()
        wa_quant(3)
        transpose_x(0)
        transpose_x(1)
        quant_x(0)
        quant_x(1)
        transpose_x(2)
        transpose_x(3)
        angle_fold()
        angle_sin()
        first_matmul(0)
        first_matmul(1)
        quant_x(2)
        quant_x(3)
        interleave_tables()
        transpose_x(4)
        transpose_x(5)
        first_matmul(2)
        first_matmul(3)
        wb_regroup(0, 1, by_vector)
        quant_cq(0)
        quant_cq(1)
        wb_quant(0, 1)
        quant_x(4)
        quant_x(5)
        make_rope(0, 0)
        make_rope(0, 1)
        transpose_x(6)
        wb_regroup(0, 0, by_vector)
        quant_cq(2)
        quant_cq(3)
        transpose_x(7)
        wb_quant(0, 0)
        rotate(0, 0)
        first_matmul(4)
        rotate(0, 1)
        make_rope(0, 2)
        first_matmul(5)
        make_rope(0, 3)
        make_nope(0, 0)
        make_nope(0, 1)
        add(0, 0, nc.gpsimd)
        quant_x(6)
        quant_x(7)
        first_matmul(6)
        rotate(0, 2)
        rotate(0, 3)
        quant_cq(4)
        quant_cq(5)
        make_rope(0, 4)
        make_rope(0, 5)
        first_matmul(7)
        add(0, 1, nc.gpsimd)
        make_nope(0, 2)
        make_nope(0, 3)
        wb_regroup(1, 1, by_scalar)
        rotate(0, 4)
        rotate(0, 5)
        quant_cq(6)
        quant_cq(7)
        make_rope(0, 6)
        make_rope(0, 7)
        add(0, 2, nc.gpsimd)
        rotate(0, 6)
        rotate(0, 7)
        wb_regroup(1, 0, by_vector)
        wb_quant(1, 1)
        wb_quant(1, 0)
        make_nope(0, 4)
        make_nope(0, 5)
        make_nope(0, 6)
        make_nope(0, 7)
        add(0, 3, nc.gpsimd)
        make_rope(1, 0)
        make_rope(1, 1)
        rotate(1, 0)
        make_nope(1, 0)
        make_rope(1, 2)
        rotate(1, 1)
        make_nope(1, 1)
        make_rope(1, 3)
        add(1, 0, nc.gpsimd)
        wb_regroup(2, 1, by_scalar)
        rotate(1, 2)
        make_nope(1, 2)
        make_rope(1, 4)
        rotate(1, 3)
        make_nope(1, 3)
        make_rope(1, 5)
        add(1, 1, nc.gpsimd)
        wb_regroup(2, 0, by_scalar)
        rotate(1, 4)
        make_nope(1, 4)
        make_rope(1, 6)
        rotate(1, 5)
        make_nope(1, 5)
        make_rope(1, 7)
        add(1, 2, nc.gpsimd)
        rotate(1, 6)
        make_nope(1, 6)
        rotate(1, 7)
        make_nope(1, 7)
        add(1, 3, nc.gpsimd)
        wb_quant(2, 1)
        wb_quant(2, 0)
        make_rope(2, 0)
        make_rope(2, 1)
        rotate(2, 0)
        make_nope(2, 0)
        make_rope(2, 2)
        rotate(2, 1)
        make_nope(2, 1)
        make_rope(2, 3)
        add(2, 0, nc.gpsimd)
        wb_regroup(3, 1, by_scalar)
        rotate(2, 2)
        make_nope(2, 2)
        make_rope(2, 4)
        rotate(2, 3)
        make_nope(2, 3)
        make_rope(2, 5)
        add(2, 1, nc.gpsimd)
        wb_regroup(3, 0, by_scalar)
        rotate(2, 4)
        make_nope(2, 4)
        make_rope(2, 6)
        rotate(2, 5)
        make_nope(2, 5)
        make_rope(2, 7)
        add(2, 2, nc.gpsimd)
        rotate(2, 6)
        make_nope(2, 6)
        rotate(2, 7)
        make_nope(2, 7)
        add(2, 3, nc.gpsimd)
        wb_quant(3, 1)
        wb_quant(3, 0)
        make_rope(3, 0)
        make_rope(3, 1)
        rotate(3, 0)
        make_nope(3, 0)
        make_rope(3, 2)
        rotate(3, 1)
        make_nope(3, 1)
        make_rope(3, 3)
        add(3, 0, nc.gpsimd)
        rotate(3, 2)
        make_nope(3, 2)
        make_rope(3, 4)
        rotate(3, 3)
        make_nope(3, 3)
        make_rope(3, 5)
        add(3, 1, nc.gpsimd)
        rotate(3, 4)
        make_nope(3, 4)
        make_rope(3, 6)
        rotate(3, 5)
        make_nope(3, 5)
        make_rope(3, 7)
        add(3, 2, nc.gpsimd)
        rotate(3, 6)
        make_nope(3, 6)
        rotate(3, 7)
        make_nope(3, 7)
        add(3, 3, nc.gpsimd)
